import numpy as np
import ml_dtypes


def mxq(x, axis, fmt="e4m3"):
    dtype, down = {"e4m3": (ml_dtypes.float8_e4m3fn, 7), "e5m2": (ml_dtypes.float8_e5m2, 14)}[fmt]
    v = np.moveaxis(np.asarray(x, np.float32).astype(ml_dtypes.bfloat16).astype(np.float64), axis, -1)
    blocks = v.reshape(v.shape[:-1] + (-1, 32))
    amax = np.abs(blocks).max(-1, keepdims=True)
    byte = np.maximum(np.where(amax > 0, np.frexp(amax)[1] - 1 + 127, 0) - down, 1)
    scale = np.exp2(byte - 127.0)
    codes = (blocks / scale).astype(np.float32).astype(dtype).astype(np.float64)
    return np.moveaxis((codes * scale).reshape(v.shape), -1, axis)


WIDE = False


def mx_kscale(k):
    if not WIDE:
        return np.ones(k)
    levels = np.array([10, -10, 5, -5, 0])
    a = np.random.permutation(np.resize(levels, k // 512 * 4)).reshape(k // 512, 4)
    idx = np.arange(k)
    return np.exp2(a[idx // 512, idx % 128 // 32])


BF16 = ml_dtypes.bfloat16


def bf(x):
    return np.asarray(x, np.float32).astype(BF16)


def f64(x):
    return np.asarray(x).astype(np.float64)


B, S, DM, DS = 2, 2048, 512, 512


def setup_inputs():
    s = mx_kscale(DM)
    return {"hidden_states": bf(np.random.standard_normal((B, S, DM)) * s),
            "positional_encodings": bf(np.random.standard_normal((B, S, DM)) * 8.0 / np.sqrt(S)),
            "W": bf(np.random.standard_normal((DS, DM)) / np.sqrt(DM) / s[None, :]),
            "b": bf(np.random.standard_normal(DS) * 0.1)}


def reference(hidden_states, positional_encodings, W, b):
    S_ = hidden_states.shape[1]
    alpha = np.exp(-np.pi / S_)
    hp = (mxq(f64(hidden_states), 2, "e4m3") @ mxq(f64(W), 1, "e4m3").T) + f64(b)
    t = np.arange(S_, dtype=np.float64)
    w = np.exp((S_ - 1.0 - t) * np.log(alpha))
    g = hp * w[None, :, None]
    return mxq(g, 1, "e4m3").transpose(0, 2, 1) @ mxq(f64(positional_encodings), 1, "e4m3")

@@ -1,0 +1,264 @@
+from contextlib import ExitStack
+import math
+
+import concourse.masks as masks
+import concourse.mybir as mybir
+
+F32 = mybir.dt.float32
+BF16 = mybir.dt.bfloat16
+U32 = mybir.dt.uint32
+U8 = mybir.dt.uint8
+I32 = mybir.dt.int32
+FP8X4 = mybir.dt.float8_e4m3fn_x4
+ALU = mybir.AluOpType
+ACT = mybir.ActivationFunctionType
+
+P = 128
+PACK = 4
+KP = P * PACK
+BATCH = 2
+SEQ = 2048
+DM = 512
+DS = 512
+CH = SEQ // KP
+NCH = BATCH * CH
+FLOPS = 2 * BATCH * SEQ * DM * DS + 2 * BATCH * DS * DM * SEQ
+
+GV = 104
+PV = 64
+
+def tile_attractorstate_v2_kernel(tc, hidden_states, positional_encodings, W, b, out):
+    nc = tc.nc
+    LOADS = [(kind, n) for n in range(NCH) for kind in ("h", "p")]
+    h_dram = hidden_states.flatten_outer_dims().rearrange("(n p j) d -> n p (j d)", p=P, j=PACK)
+    p_dram = positional_encodings.flatten_outer_dims().rearrange("(n p j) m -> n p (j m)", p=P, j=PACK)
+
+    with ExitStack() as ctx:
+        res = ctx.enter_context(tc.tile_pool(name="res", bufs=1))
+        work2 = ctx.enter_context(tc.tile_pool(name="work2", bufs=2))
+        work3 = ctx.enter_context(tc.tile_pool(name="work3", bufs=3))
+        work4 = ctx.enter_context(tc.tile_pool(name="work4", bufs=4))
+        tpool = ctx.enter_context(tc.psum_pool(name="tpool", bufs=2))
+        spool = ctx.enter_context(tc.psum_pool(name="spool", bufs=2))
+        apool = ctx.enter_context(tc.psum_pool(name="apool", bufs=1))
+        ctx.enter_context(tc.manual_schedule())
+
+        brow = res.tile([P, DS], BF16, name="brow")
+        nc.vector.memset(brow[:], 0.0)
+        ones = res.tile([P, P], BF16, name="ones")
+        nc.vector.memset(ones[:], 1.0)
+        nc.sync.dma_start(out=brow[0:1, :], in_=b.unsqueeze(0))
+        w_sb = res.tile([P, PACK * DM], BF16, name="w_sb")
+        nc.sync.dma_start(out=w_sb[:].rearrange("p (r d) -> p r d", r=PACK),
+                          in_=W.rearrange("(r p) d -> p r d", p=P))
+        h_sb = []
+        p_sb = []
+        for n in range(NCH):
+            h_sb.append(res.tile([P, PACK * DM], BF16, name="h_sb%d" % n))
+            p_sb.append(res.tile([P, PACK, DM], BF16, name="p_sb%d" % n))
+        for kind, n in LOADS:
+            if kind == "h":
+                nc.sync.dma_start(out=h_sb[n][:], in_=h_dram[n])
+            else:
+                nc.sync.dma_start(out=p_sb[n][:].rearrange("p j m -> p (j m)"), in_=p_dram[n])
+
+        ident = res.tile([P, P], F32, name="ident")
+        masks.make_identity(nc, ident[:])
+        idx = res.tile([P, CH * PACK], I32, name="idx")
+        nc.gpsimd.iota(idx[:], pattern=[[KP, CH], [1, PACK]], base=1 - SEQ, channel_multiplier=PACK)
+        idxf = res.tile([P, CH * PACK], F32, name="idxf")
+        nc.vector.tensor_copy(out=idxf[:], in_=idx[:])
+        wcol = res.tile([P, CH * PACK], F32, name="wcol")
+        nc.scalar.activation(out=wcol[:], in_=idxf[:], func=ACT.Exp, scale=math.pi / SEQ)
+
+        psb = spool.tile([P, DS], F32, name="ps1")
+        nc.tensor.matmul(out=psb[:], lhsT=ones[:], rhs=brow[:], start=True, stop=True)
+        b_bc = res.tile([P, DS], F32, name="b_bc")
+        nc.vector.tensor_copy(out=b_bc[:], in_=psb[:])
+        bw = res.tile([P, CH * PACK, DS], F32, name="bw")
+
+        def make_bw(k, eng):
+            if eng == "v":
+                nc.vector.tensor_scalar(out=bw[:, k, :], in0=b_bc[:], scalar1=wcol[:, k:k + 1], scalar2=None,
+                                        op0=ALU.mult)
+            elif eng == "s":
+                nc.scalar.activation(out=bw[:, k, :], in_=b_bc[:], func=ACT.Copy, scale=wcol[:, k:k + 1])
+            else:
+                nc.gpsimd.tensor_scalar(out=bw[:, k, :], in0=b_bc[:], scalar1=wcol[:, k:k + 1], scalar2=0.0,
+                                        op0=ALU.mult, op1=ALU.add)
+
+        def transposes(src):
+            banks = []
+            sv = src[:].bitcast(F32)
+            for half in range(2):
+                tp = tpool.tile([P, 2, 2, P], F32, name="tp")
+                for a in range(2):
+                    for u in range(2):
+                        col = 256 * (2 * half + a) + P * u
+                        nc.tensor.transpose(tp[:, a, u, :], sv[:, col:col + P], ident[:])
+                banks.append(tp)
+            return banks
+
+        def copy_out_words(banks, grp, engines):
+            gv = grp[:].bitcast(F32)
+            for half in range(2):
+                dst = gv[:, 512 * half:512 * half + 512].rearrange("q (a p u) -> q a p u", a=2, u=2)
+                srcv = banks[half][:].rearrange("q a u p -> q a p u")
+                if engines[half] == "v":
+                    nc.vector.tensor_copy(out=dst, in_=srcv)
+                else:
+                    nc.scalar.copy(out=dst, in_=srcv)
+
+        def quantise(grp_flat, codes, scales):
+            nc.vector.quantize_mx(out=codes.bitcast(FP8X4), scales=scales, in_=grp_flat)
+
+        def regroup(eng, dst, src, lo, hi):
+            if hi <= lo:
+                return
+            if eng == "g":
+                nc.gpsimd.tensor_scalar(out=dst[:, lo:hi, :], in0=src[:, :, lo:hi].rearrange("p t c -> p c t"),
+                                        scalar1=1.0, scalar2=0.0, op0=ALU.mult, op1=ALU.add)
+                return
+            d = dst[:, lo:hi, :].rearrange("p (c i) t -> p c t i", i=4)
+            s = src[:, :, lo:hi].rearrange("p t (c i) -> p c t i", i=4)
+            if eng == "v":
+                nc.vector.tensor_copy(out=d, in_=s)
+            else:
+                nc.scalar.copy(out=d, in_=s)
+
+        st = {}
+
+        def T(n):
+            st["tp", n] = transposes(h_sb[n])
+
+        def HC(n, engines):
+            hgrp = work2.tile([P, PACK * KP], BF16, name="hgrp", align_bytes=64)
+            copy_out_words(st["tp", n], hgrp, engines)
+            st["hgrp", n] = hgrp
+
+        def HQ(n):
+            hq = work2.tile([P, KP], U32, name="hq", align_bytes=64)
+            hs = work2.tile([P, KP], U8, name="hs", align_bytes=64)
+            quantise(st["hgrp", n][:], hq[:], hs[:])
+            st["hq", n] = (hq, hs)
+
+        def S1(n, j):
+            hq, hs = st["hq", n]
+            ps = spool.tile([P, DS], F32, name="ps1")
+            nc.tensor.matmul_mx(out=ps[:], lhsT=hq[:, P * j:P * j + P].bitcast(FP8X4),
+                                lhsT_scale=hs[:, P * j:P * j + P],
+                                rhs=wq[:].bitcast(FP8X4), rhs_scale=ws[:], start=True, stop=True)
+            st["ps", n, j] = ps
+
+        def E(n, j):
+            if j == 0:
+                st["glin", n] = work3.tile([P, PACK, DS], BF16, name="glin")
+            k = PACK * (n % CH) + j
+            nc.vector.scalar_tensor_tensor(out=st["glin", n][:, j, :], in0=st["ps", n, j][:],
+                                           scalar=wcol[:, k:k + 1], in1=bw[:, k, :],
+                                           op0=ALU.mult, op1=ALU.add)
+
+        def GR(n, eng, lo, hi):
+            if ("ggrp", n) not in st:
+                st["ggrp", n] = work2.tile([P, DS, PACK], BF16, name="ggrp", align_bytes=64)
+            regroup(eng, st["ggrp", n], st["glin", n], lo, hi)
+
+        def GQ(n, lo, hi):
+            if ("gq", n) not in st:
+                gq = work2.tile([P, DS], U32, name="gq", align_bytes=64)
+                gs = work2.tile([P, DS], U8, name="gs", align_bytes=64)
+                st["gq", n] = (gq, gs)
+            gq, gs = st["gq", n]
+            quantise(st["ggrp", n][:, lo:hi, :].rearrange("p s j -> p (s j)"), gq[:, lo:hi], gs[:, lo:hi])
+
+        def PR(n, eng, lo, hi):
+            if ("pgrp", n) not in st:
+                st["pgrp", n] = work2.tile([P, DM, PACK], BF16, name="pgrp", align_bytes=64)
+            regroup(eng, st["pgrp", n], p_sb[n], lo, hi)
+
+        def PQ(n):
+            pq = work4.tile([P, DM], U32, name="pq", align_bytes=64)
+            pscale = work4.tile([P, DM], U8, name="pscale", align_bytes=64)
+            quantise(st["pgrp", n][:].rearrange("p m j -> p (m j)"), pq[:], pscale[:])
+            st["pq", n] = (pq, pscale)
+
+        def S2(n, r):
+            c = n % CH
+            gq, gs = st["gq", n]
+            pq, pscale = st["pq", n]
+            if c == 0:
+                st["acc", n // CH, r] = apool.tile([P, DM], F32, name="acc%d" % r)
+            nc.tensor.matmul_mx(out=st["acc", n // CH, r][:],
+                                lhsT=gq[:, P * r:P * r + P].bitcast(FP8X4),
+                                lhsT_scale=gs[:, P * r:P * r + P],
+                                rhs=pq[:].bitcast(FP8X4), rhs_scale=pscale[:],
+                                start=(c == 0), stop=(c == CH - 1))
+
+        def O(i, r, eng):
+            osb = work4.tile([P, DM], F32, name="osb")
+            if eng == "s":
+                nc.scalar.copy(out=osb[:], in_=st["acc", i, r][:])
+            else:
+                nc.vector.tensor_copy(out=osb[:], in_=st["acc", i, r][:])
+            nc.sync.dma_start(out=out[i, P * r:P * r + P, :], in_=osb[:])
+
+        for k in range(4):
+            make_bw(k, "v")
+        wbanks = transposes(w_sb)
+        wgrp = res.tile([P, PACK * KP], BF16, name="wgrp", align_bytes=64)
+        copy_out_words(wbanks, wgrp, ["s", "v"])
+        T(0)
+        wq = res.tile([P, DS], U32, name="wq", align_bytes=64)
+        ws = res.tile([P, DS], U8, name="ws", align_bytes=64)
+        quantise(wgrp[:], wq[:], ws[:])
+        HC(0, ["s", "v"])
+        for k in range(4, 8):
+            make_bw(k, "v")
+        HQ(0)
+        T(1)
+        PR(0, "s", 0, DM - PV)
+        PR(0, "v", DM - PV, DM)
+        for k in range(8, 16):
+            make_bw(k, "v")
+
+        for n in range(NCH):
+            if n + 1 < NCH:
+                HC(n + 1, ["s", "s"])
+            if n >= 1:
+                GR(n - 1, "s", 0, DS - GV)
+            S1(n, 0)
+            S1(n, 1)
+            if n >= 2:
+                for r in range(PACK):
+                    S2(n - 2, r)
+            E(n, 0)
+            S1(n, 2)
+            E(n, 1)
+            S1(n, 3)
+            if n + 2 < NCH:
+                T(n + 2)
+            if n == CH + 1:
+                for r in range(PACK):
+                    O(0, r, "sv"[r % 2])
+            if n + 1 < NCH:
+                HQ(n + 1)
+            PQ(n)
+            E(n, 2)
+            E(n, 3)
+            if n >= 1:
+                GQ(n - 1, 0, DS)
+            if n + 1 < NCH:
+                GR(n, "v", DS - GV, DS)
+                PR(n + 1, "s", 0, DM - PV)
+                PR(n + 1, "v", DM - PV, DM)
+
+        last = NCH - 1
+        for r in range(PACK):
+            S2(last - 1, r)
+        for r in range(PACK):
+            GR(last, "vsvs"[r], P * r, P * r + P)
+        for r in range(PACK):
+            GQ(last, P * r, P * r + P)
+            S2(last, r)
+        for r in range(PACK):
+            O(1, r, "sv"[r % 2])

@@ -24,8 +24,8 @@ CH = SEQ // KP
 NCH = BATCH * CH
 FLOPS = 2 * BATCH * SEQ * DM * DS + 2 * BATCH * DS * DM * SEQ
 
-GV = 104
-PV = 64
+PG = 448
+NG = 1
 
 def tile_attractorstate_v2_kernel(tc, hidden_states, positional_encodings, W, b, out):
     nc = tc.nc
@@ -202,6 +202,20 @@ def tile_attractorstate_v2_kernel(tc, hidden_states, positional_encodings, W, b,
                 nc.vector.tensor_copy(out=osb[:], in_=st["acc", i, r][:])
             nc.sync.dma_start(out=out[i, P * r:P * r + P, :], in_=osb[:])
 
+        def PRall(n):
+            step = PG // NG
+            for q in range(NG):
+                PR(n, "g", step * q, step * q + step)
+            PR(n, "s", PG, DM)
+
+        bw_next = [4 + 4]
+
+        def bw_on_scalar(count):
+            for q in range(count):
+                if bw_next[0] < CH * PACK:
+                    make_bw(bw_next[0], "s")
+                    bw_next[0] = bw_next[0] + 1
+
         for k in range(4):
             make_bw(k, "v")
         wbanks = transposes(w_sb)
@@ -212,20 +226,18 @@ def tile_attractorstate_v2_kernel(tc, hidden_states, positional_encodings, W, b,
         ws = res.tile([P, DS], U8, name="ws", align_bytes=64)
         quantise(wgrp[:], wq[:], ws[:])
         HC(0, ["s", "v"])
-        for k in range(4, 8):
-            make_bw(k, "v")
         HQ(0)
         T(1)
-        PR(0, "s", 0, DM - PV)
-        PR(0, "v", DM - PV, DM)
-        for k in range(8, 16):
+        PR(0, "s", 0, DM)
+        for k in range(4, 4 + 4):
             make_bw(k, "v")
+        HC(1, ["s", "s"])
+        bw_on_scalar(3)
+        PRall(1)
 
+        last = NCH - 1
+        bw_plan = [3,3,3]
         for n in range(NCH):
-            if n + 1 < NCH:
-                HC(n + 1, ["s", "s"])
-            if n >= 1:
-                GR(n - 1, "s", 0, DS - GV)
             S1(n, 0)
             S1(n, 1)
             if n >= 2:
@@ -237,22 +249,29 @@ def tile_attractorstate_v2_kernel(tc, hidden_states, positional_encodings, W, b,
             S1(n, 3)
             if n + 2 < NCH:
                 T(n + 2)
-            if n == CH + 1:
-                for r in range(PACK):
-                    O(0, r, "sv"[r % 2])
-            if n + 1 < NCH:
-                HQ(n + 1)
-            PQ(n)
+            if n == last:
+                GQ(n - 1, 0, DS)
             E(n, 2)
             E(n, 3)
-            if n >= 1:
+            if n == CH + 1:
+                for r in range(PACK):
+                    O(0, r, "ssss"[r])
+            if n < last:
+                GR(n, "s", 0, DS)
+                HQ(n + 1)
+            if 1 <= n < last:
                 GQ(n - 1, 0, DS)
-            if n + 1 < NCH:
-                GR(n, "v", DS - GV, DS)
-                PR(n + 1, "s", 0, DM - PV)
-                PR(n + 1, "v", DM - PV, DM)
+            if n < last:
+                PQ(n)
+            if n == last - 1:
+                PQ(last)
+            if n + 2 < NCH:
+                HC(n + 2, ["s", "s"])
+            if n < len(bw_plan):
+                bw_on_scalar(bw_plan[n])
+            if n + 2 < NCH:
+                PRall(n + 2)
 
-        last = NCH - 1
         for r in range(PACK):
             S2(last - 1, r)
         for r in range(PACK):

@@ -24,8 +24,7 @@ CH = SEQ // KP
 NCH = BATCH * CH
 FLOPS = 2 * BATCH * SEQ * DM * DS + 2 * BATCH * DS * DM * SEQ
 
-PG = 448
-NG = 1
+PG = 416
 
 def tile_attractorstate_v2_kernel(tc, hidden_states, positional_encodings, W, b, out):
     nc = tc.nc
@@ -64,28 +63,19 @@ def tile_attractorstate_v2_kernel(tc, hidden_states, positional_encodings, W, b,
 
         ident = res.tile([P, P], F32, name="ident")
         masks.make_identity(nc, ident[:])
-        idx = res.tile([P, CH * PACK], I32, name="idx")
-        nc.gpsimd.iota(idx[:], pattern=[[KP, CH], [1, PACK]], base=1 - SEQ, channel_multiplier=PACK)
-        idxf = res.tile([P, CH * PACK], F32, name="idxf")
+        idx = res.tile([P, CH], I32, name="idx")
+        nc.gpsimd.iota(idx[:], pattern=[[KP, CH]], base=1 - SEQ, channel_multiplier=PACK)
+        idxf = res.tile([P, CH], F32, name="idxf")
         nc.vector.tensor_copy(out=idxf[:], in_=idx[:])
-        wcol = res.tile([P, CH * PACK], F32, name="wcol")
-        nc.scalar.activation(out=wcol[:], in_=idxf[:], func=ACT.Exp, scale=math.pi / SEQ)
+        wpc = res.tile([P, CH], F32, name="wpc")
+        nc.scalar.activation(out=wpc[:], in_=idxf[:], func=ACT.Exp, scale=math.pi / SEQ)
+        ej = [math.exp(j * math.pi / SEQ) for j in range(PACK)]
 
         psb = spool.tile([P, DS], F32, name="ps1")
         nc.tensor.matmul(out=psb[:], lhsT=ones[:], rhs=brow[:], start=True, stop=True)
         b_bc = res.tile([P, DS], F32, name="b_bc")
         nc.vector.tensor_copy(out=b_bc[:], in_=psb[:])
-        bw = res.tile([P, CH * PACK, DS], F32, name="bw")
-
-        def make_bw(k, eng):
-            if eng == "v":
-                nc.vector.tensor_scalar(out=bw[:, k, :], in0=b_bc[:], scalar1=wcol[:, k:k + 1], scalar2=None,
-                                        op0=ALU.mult)
-            elif eng == "s":
-                nc.scalar.activation(out=bw[:, k, :], in_=b_bc[:], func=ACT.Copy, scale=wcol[:, k:k + 1])
-            else:
-                nc.gpsimd.tensor_scalar(out=bw[:, k, :], in0=b_bc[:], scalar1=wcol[:, k:k + 1], scalar2=0.0,
-                                        op0=ALU.mult, op1=ALU.add)
+        be = res.tile([P, PACK, DS], F32, name="be")
 
         def transposes(src):
             banks = []
@@ -112,7 +102,7 @@ def tile_attractorstate_v2_kernel(tc, hidden_states, positional_encodings, W, b,
         def quantise(grp_flat, codes, scales):
             nc.vector.quantize_mx(out=codes.bitcast(FP8X4), scales=scales, in_=grp_flat)
 
-        def regroup(eng, dst, src, lo, hi):
+        def regroup(eng, dst, src, lo, hi, scale):
             if hi <= lo:
                 return
             if eng == "g":
@@ -121,10 +111,15 @@ def tile_attractorstate_v2_kernel(tc, hidden_states, positional_encodings, W, b,
                 return
             d = dst[:, lo:hi, :].rearrange("p (c i) t -> p c t i", i=4)
             s = src[:, :, lo:hi].rearrange("p t (c i) -> p c t i", i=4)
-            if eng == "v":
-                nc.vector.tensor_copy(out=d, in_=s)
+            if scale is None:
+                if eng == "v":
+                    nc.vector.tensor_copy(out=d, in_=s)
+                else:
+                    nc.scalar.copy(out=d, in_=s)
+            elif eng == "v":
+                nc.vector.tensor_scalar(out=d, in0=s, scalar1=scale, scalar2=None, op0=ALU.mult)
             else:
-                nc.scalar.copy(out=d, in_=s)
+                nc.scalar.activation(out=d, in_=s, func=ACT.Copy, scale=scale)
 
         st = {}
 
@@ -152,16 +147,15 @@ def tile_attractorstate_v2_kernel(tc, hidden_states, positional_encodings, W, b,
 
         def E(n, j):
             if j == 0:
-                st["glin", n] = work3.tile([P, PACK, DS], BF16, name="glin")
-            k = PACK * (n % CH) + j
+                st["glin", n] = work3.tile([P, PACK, DS], F32, name="glin")
             nc.vector.scalar_tensor_tensor(out=st["glin", n][:, j, :], in0=st["ps", n, j][:],
-                                           scalar=wcol[:, k:k + 1], in1=bw[:, k, :],
-                                           op0=ALU.mult, op1=ALU.add)
+                                           scalar=ej[j], in1=be[:, j, :], op0=ALU.mult, op1=ALU.add)
 
         def GR(n, eng, lo, hi):
             if ("ggrp", n) not in st:
                 st["ggrp", n] = work2.tile([P, DS, PACK], BF16, name="ggrp", align_bytes=64)
-            regroup(eng, st["ggrp", n], st["glin", n], lo, hi)
+            c = n % CH
+            regroup(eng, st["ggrp", n], st["glin", n], lo, hi, wpc[:, c:c + 1])
 
         def GQ(n, lo, hi):
             if ("gq", n) not in st:
@@ -174,7 +168,7 @@ def tile_attractorstate_v2_kernel(tc, hidden_states, positional_encodings, W, b,
         def PR(n, eng, lo, hi):
             if ("pgrp", n) not in st:
                 st["pgrp", n] = work2.tile([P, DM, PACK], BF16, name="pgrp", align_bytes=64)
-            regroup(eng, st["pgrp", n], p_sb[n], lo, hi)
+            regroup(eng, st["pgrp", n], p_sb[n], lo, hi, None)
 
         def PQ(n):
             pq = work4.tile([P, DM], U32, name="pq", align_bytes=64)
@@ -203,24 +197,14 @@ def tile_attractorstate_v2_kernel(tc, hidden_states, positional_encodings, W, b,
             nc.sync.dma_start(out=out[i, P * r:P * r + P, :], in_=osb[:])
 
         def PRall(n):
-            step = PG // NG
-            for q in range(NG):
-                PR(n, "g", step * q, step * q + step)
+            PR(n, "g", 0, PG)
             PR(n, "s", PG, DM)
 
-        bw_next = [4 + 4]
-
-        def bw_on_scalar(count):
-            for q in range(count):
-                if bw_next[0] < CH * PACK:
-                    make_bw(bw_next[0], "s")
-                    bw_next[0] = bw_next[0] + 1
-
-        for k in range(4):
-            make_bw(k, "v")
+        for j in range(PACK):
+            nc.vector.tensor_scalar(out=be[:, j, :], in0=b_bc[:], scalar1=ej[j], scalar2=None, op0=ALU.mult)
         wbanks = transposes(w_sb)
         wgrp = res.tile([P, PACK * KP], BF16, name="wgrp", align_bytes=64)
-        copy_out_words(wbanks, wgrp, ["s", "v"])
+        copy_out_words(wbanks, wgrp, ["s", "s"])
         T(0)
         wq = res.tile([P, DS], U32, name="wq", align_bytes=64)
         ws = res.tile([P, DS], U8, name="ws", align_bytes=64)
@@ -229,14 +213,10 @@ def tile_attractorstate_v2_kernel(tc, hidden_states, positional_encodings, W, b,
         HQ(0)
         T(1)
         PR(0, "s", 0, DM)
-        for k in range(4, 4 + 4):
-            make_bw(k, "v")
         HC(1, ["s", "s"])
-        bw_on_scalar(3)
         PRall(1)
 
         last = NCH - 1
-        bw_plan = [3,3,3]
         for n in range(NCH):
             S1(n, 0)
             S1(n, 1)
@@ -267,9 +247,6 @@ def tile_attractorstate_v2_kernel(tc, hidden_states, positional_encodings, W, b,
                 PQ(last)
             if n + 2 < NCH:
                 HC(n + 2, ["s", "s"])
-            if n < len(bw_plan):
-                bw_on_scalar(bw_plan[n])
-            if n + 2 < NCH:
                 PRall(n + 2)
 
         for r in range(PACK):

@@ -22,15 +22,18 @@ DM = 512
 DS = 512
 CH = SEQ // KP
 NCH = BATCH * CH
+HALF = DS // 2
 FLOPS = 2 * BATCH * SEQ * DM * DS + 2 * BATCH * DS * DM * SEQ
 
-PG = 416
+PG = 384
+PG1 = 256
+
 
 def tile_attractorstate_v2_kernel(tc, hidden_states, positional_encodings, W, b, out):
     nc = tc.nc
-    LOADS = [(kind, n) for n in range(NCH) for kind in ("h", "p")]
     h_dram = hidden_states.flatten_outer_dims().rearrange("(n p j) d -> n p (j d)", p=P, j=PACK)
     p_dram = positional_encodings.flatten_outer_dims().rearrange("(n p j) m -> n p (j m)", p=P, j=PACK)
+    last = NCH - 1
 
     with ExitStack() as ctx:
         res = ctx.enter_context(tc.tile_pool(name="res", bufs=1))
@@ -47,19 +50,36 @@ def tile_attractorstate_v2_kernel(tc, hidden_states, positional_encodings, W, b,
         ones = res.tile([P, P], BF16, name="ones")
         nc.vector.memset(ones[:], 1.0)
         nc.sync.dma_start(out=brow[0:1, :], in_=b.unsqueeze(0))
-        w_sb = res.tile([P, PACK * DM], BF16, name="w_sb")
-        nc.sync.dma_start(out=w_sb[:].rearrange("p (r d) -> p r d", r=PACK),
-                          in_=W.rearrange("(r p) d -> p r d", p=P))
-        h_sb = []
-        p_sb = []
-        for n in range(NCH):
-            h_sb.append(res.tile([P, PACK * DM], BF16, name="h_sb%d" % n))
-            p_sb.append(res.tile([P, PACK, DM], BF16, name="p_sb%d" % n))
-        for kind, n in LOADS:
-            if kind == "h":
-                nc.sync.dma_start(out=h_sb[n][:], in_=h_dram[n])
-            else:
-                nc.sync.dma_start(out=p_sb[n][:].rearrange("p j m -> p (j m)"), in_=p_dram[n])
+        w_half = []
+        for h in range(2):
+            wt = res.tile([P, 2 * DM], BF16, name="w_half%d" % h)
+            nc.sync.dma_start(out=wt[:].rearrange("p (r d) -> p r d", r=2),
+                              in_=W[2 * P * h:2 * P * h + 2 * P, :].rearrange("(r p) d -> p r d", p=P))
+            w_half.append(wt[:].bitcast(F32))
+        h_half = {}
+        p_sb = {}
+
+        def load_h(n, pieces):
+            width = PACK * DM // pieces
+            for q in range(pieces):
+                ht = res.tile([P, width], BF16, name="h_sb%d_%d" % (n, q))
+                nc.sync.dma_start(out=ht[:], in_=h_dram[n][:, width * q:width * q + width])
+                words = ht[:].bitcast(F32)
+                for h in range(2 // pieces):
+                    h_half[n, q * (2 // pieces) + h] = words[:, DM * h:DM * h + DM]
+
+        def load_p(n):
+            pt = res.tile([P, PACK, DM], BF16, name="p_sb%d" % n)
+            nc.sync.dma_start(out=pt[:].rearrange("p j m -> p (j m)"), in_=p_dram[n])
+            p_sb[n] = pt
+
+        load_h(0, 2)
+        load_h(1, 1)
+        load_p(0)
+        load_p(1)
+        for n in range(2, NCH):
+            load_h(n, 1)
+            load_p(n)
 
         ident = res.tile([P, P], F32, name="ident")
         masks.make_identity(nc, ident[:])
@@ -73,89 +93,86 @@ def tile_attractorstate_v2_kernel(tc, hidden_states, positional_encodings, W, b,
 
         psb = spool.tile([P, DS], F32, name="ps1")
         nc.tensor.matmul(out=psb[:], lhsT=ones[:], rhs=brow[:], start=True, stop=True)
-        b_bc = res.tile([P, DS], F32, name="b_bc")
-        nc.vector.tensor_copy(out=b_bc[:], in_=psb[:])
         be = res.tile([P, PACK, DS], F32, name="be")
+        nc.vector.tensor_copy(out=be[:, 0, :], in_=psb[:])
 
-        def transposes(src):
-            banks = []
-            sv = src[:].bitcast(F32)
-            for half in range(2):
-                tp = tpool.tile([P, 2, 2, P], F32, name="tp")
-                for a in range(2):
-                    for u in range(2):
-                        col = 256 * (2 * half + a) + P * u
-                        nc.tensor.transpose(tp[:, a, u, :], sv[:, col:col + P], ident[:])
-                banks.append(tp)
-            return banks
+        def make_be(j):
+            nc.vector.tensor_scalar(out=be[:, j, :], in0=be[:, 0, :], scalar1=ej[j], scalar2=None, op0=ALU.mult)
 
-        def copy_out_words(banks, grp, engines):
-            gv = grp[:].bitcast(F32)
-            for half in range(2):
-                dst = gv[:, 512 * half:512 * half + 512].rearrange("q (a p u) -> q a p u", a=2, u=2)
-                srcv = banks[half][:].rearrange("q a u p -> q a p u")
-                if engines[half] == "v":
-                    nc.vector.tensor_copy(out=dst, in_=srcv)
-                else:
-                    nc.scalar.copy(out=dst, in_=srcv)
+        st = {}
+
+        def transpose_half(key, words):
+            tp = tpool.tile([P, 2, 2, P], F32, name="tp")
+            for a in range(2):
+                for u in range(2):
+                    col = 2 * P * a + P * u
+                    nc.tensor.transpose(tp[:, a, u, :], words[:, col:col + P], ident[:])
+            st["tp", key] = tp
+
+        def copy_half(key, grp, h, eng):
+            dst = grp[:].bitcast(F32)[:, DM * h:DM * h + DM].rearrange("q (a p u) -> q a p u", a=2, u=2)
+            src = st["tp", key][:].rearrange("q a u p -> q a p u")
+            if eng == "v":
+                nc.vector.tensor_copy(out=dst, in_=src)
+            else:
+                nc.scalar.copy(out=dst, in_=src)
 
         def quantise(grp_flat, codes, scales):
             nc.vector.quantize_mx(out=codes.bitcast(FP8X4), scales=scales, in_=grp_flat)
 
-        def regroup(eng, dst, src, lo, hi, scale):
-            if hi <= lo:
-                return
-            if eng == "g":
-                nc.gpsimd.tensor_scalar(out=dst[:, lo:hi, :], in0=src[:, :, lo:hi].rearrange("p t c -> p c t"),
-                                        scalar1=1.0, scalar2=0.0, op0=ALU.mult, op1=ALU.add)
-                return
+        def T(n, h):
+            transpose_half((n, h), h_half[n, h])
+
+        def HC(n, h, eng):
+            if h == 0:
+                st["hgrp", n] = work2.tile([P, PACK * KP], BF16, name="hgrp", align_bytes=64)
+            copy_half((n, h), st["hgrp", n], h, eng)
+
+        def HQ(n, lo, hi):
+            if ("hq", n) not in st:
+                hq = work2.tile([P, KP], U32, name="hq", align_bytes=64)
+                hs = work2.tile([P, KP], U8, name="hs", align_bytes=64)
+                st["hq", n] = (hq, hs)
+            hq, hs = st["hq", n]
+            quantise(st["hgrp", n][:, PACK * lo:PACK * hi], hq[:, lo:hi], hs[:, lo:hi])
+
+        def S1(n, j, ps, lo, hi):
+            hq, hs = st["hq", n]
+            nc.tensor.matmul_mx(out=ps, lhsT=hq[:, P * j:P * j + P].bitcast(FP8X4),
+                                lhsT_scale=hs[:, P * j:P * j + P],
+                                rhs=wq[:, lo:hi].bitcast(FP8X4), rhs_scale=ws[:, lo:hi], start=True, stop=True)
+
+        def S1full(n, j):
+            ps = spool.tile([P, DS], F32, name="ps1")
+            S1(n, j, ps[:], 0, DS)
+            st["ps", n, j] = ps[:]
+
+        def S1pair(n, j, lo):
+            ps = spool.tile([P, DS], F32, name="ps1")
+            for e in range(2):
+                S1(n, j + e, ps[:, HALF * e:HALF * e + HALF], lo, lo + HALF)
+                st["ps", n, j + e] = ps[:, HALF * e:HALF * e + HALF]
+
+        def E(n, j, lo, hi):
+            if ("glin", n) not in st:
+                st["glin", n] = work3.tile([P, PACK, DS], F32, name="glin")
+            nc.vector.scalar_tensor_tensor(out=st["glin", n][:, j, lo:hi], in0=st["ps", n, j],
+                                           scalar=ej[j], in1=be[:, j, lo:hi], op0=ALU.mult, op1=ALU.add)
+
+        def views(dst, src, lo, hi):
             d = dst[:, lo:hi, :].rearrange("p (c i) t -> p c t i", i=4)
             s = src[:, :, lo:hi].rearrange("p t (c i) -> p c t i", i=4)
-            if scale is None:
-                if eng == "v":
-                    nc.vector.tensor_copy(out=d, in_=s)
-                else:
-                    nc.scalar.copy(out=d, in_=s)
-            elif eng == "v":
-                nc.vector.tensor_scalar(out=d, in0=s, scalar1=scale, scalar2=None, op0=ALU.mult)
-            else:
-                nc.scalar.activation(out=d, in_=s, func=ACT.Copy, scale=scale)
-
-        st = {}
-
-        def T(n):
-            st["tp", n] = transposes(h_sb[n])
-
-        def HC(n, engines):
-            hgrp = work2.tile([P, PACK * KP], BF16, name="hgrp", align_bytes=64)
-            copy_out_words(st["tp", n], hgrp, engines)
-            st["hgrp", n] = hgrp
-
-        def HQ(n):
-            hq = work2.tile([P, KP], U32, name="hq", align_bytes=64)
-            hs = work2.tile([P, KP], U8, name="hs", align_bytes=64)
-            quantise(st["hgrp", n][:], hq[:], hs[:])
-            st["hq", n] = (hq, hs)
-
-        def S1(n, j):
-            hq, hs = st["hq", n]
-            ps = spool.tile([P, DS], F32, name="ps1")
-            nc.tensor.matmul_mx(out=ps[:], lhsT=hq[:, P * j:P * j + P].bitcast(FP8X4),
-                                lhsT_scale=hs[:, P * j:P * j + P],
-                                rhs=wq[:].bitcast(FP8X4), rhs_scale=ws[:], start=True, stop=True)
-            st["ps", n, j] = ps
-
-        def E(n, j):
-            if j == 0:
-                st["glin", n] = work3.tile([P, PACK, DS], F32, name="glin")
-            nc.vector.scalar_tensor_tensor(out=st["glin", n][:, j, :], in0=st["ps", n, j][:],
-                                           scalar=ej[j], in1=be[:, j, :], op0=ALU.mult, op1=ALU.add)
+            return d, s
 
         def GR(n, eng, lo, hi):
             if ("ggrp", n) not in st:
                 st["ggrp", n] = work2.tile([P, DS, PACK], BF16, name="ggrp", align_bytes=64)
+            d, s = views(st["ggrp", n], st["glin", n], lo, hi)
             c = n % CH
-            regroup(eng, st["ggrp", n], st["glin", n], lo, hi, wpc[:, c:c + 1])
+            if eng == "v":
+                nc.vector.tensor_scalar(out=d, in0=s, scalar1=wpc[:, c:c + 1], scalar2=None, op0=ALU.mult)
+            else:
+                nc.scalar.activation(out=d, in_=s, func=ACT.Copy, scale=wpc[:, c:c + 1])
 
         def GQ(n, lo, hi):
             if ("gq", n) not in st:
@@ -168,7 +185,16 @@ def tile_attractorstate_v2_kernel(tc, hidden_states, positional_encodings, W, b,
         def PR(n, eng, lo, hi):
             if ("pgrp", n) not in st:
                 st["pgrp", n] = work2.tile([P, DM, PACK], BF16, name="pgrp", align_bytes=64)
-            regroup(eng, st["pgrp", n], p_sb[n], lo, hi, None)
+            if eng == "g":
+                nc.gpsimd.tensor_scalar(out=st["pgrp", n][:, lo:hi, :],
+                                        in0=p_sb[n][:, :, lo:hi].rearrange("p t c -> p c t"),
+                                        scalar1=1.0, scalar2=0.0, op0=ALU.mult, op1=ALU.add)
+                return
+            d, s = views(st["pgrp", n], p_sb[n], lo, hi)
+            if eng == "v":
+                nc.vector.tensor_copy(out=d, in_=s)
+            else:
+                nc.scalar.copy(out=d, in_=s)
 
         def PQ(n):
             pq = work4.tile([P, DM], U32, name="pq", align_bytes=64)
@@ -196,65 +222,95 @@ def tile_attractorstate_v2_kernel(tc, hidden_states, positional_encodings, W, b,
                 nc.vector.tensor_copy(out=osb[:], in_=st["acc", i, r][:])
             nc.sync.dma_start(out=out[i, P * r:P * r + P, :], in_=osb[:])
 
-        def PRall(n):
-            PR(n, "g", 0, PG)
-            PR(n, "s", PG, DM)
-
-        for j in range(PACK):
-            nc.vector.tensor_scalar(out=be[:, j, :], in0=b_bc[:], scalar1=ej[j], scalar2=None, op0=ALU.mult)
-        wbanks = transposes(w_sb)
         wgrp = res.tile([P, PACK * KP], BF16, name="wgrp", align_bytes=64)
-        copy_out_words(wbanks, wgrp, ["s", "s"])
-        T(0)
         wq = res.tile([P, DS], U32, name="wq", align_bytes=64)
         ws = res.tile([P, DS], U8, name="ws", align_bytes=64)
+        for h in range(2):
+            transpose_half(("w", h), w_half[h])
+        for h in range(2):
+            copy_half(("w", h), wgrp, h, "s")
+        T(0, 0)
+        T(0, 1)
         quantise(wgrp[:], wq[:], ws[:])
-        HC(0, ["s", "v"])
-        HQ(0)
-        T(1)
+        HC(0, 0, "s")
+        HC(0, 1, "s")
+        make_be(1)
+        HQ(0, 0, HALF)
+        make_be(2)
+        HQ(0, HALF, KP)
+        make_be(3)
+        T(1, 0)
+        T(1, 1)
+        HC(1, 0, "s")
+        HC(1, 1, "s")
+        S1full(0, 0)
+        S1full(0, 1)
         PR(0, "s", 0, DM)
-        HC(1, ["s", "s"])
-        PRall(1)
+        PR(1, "g", 0, PG1)
 
-        last = NCH - 1
-        for n in range(NCH):
-            S1(n, 0)
-            S1(n, 1)
+        for n in range(last):
+            if n > 0:
+                S1full(n, 0)
+                S1full(n, 1)
             if n >= 2:
                 for r in range(PACK):
                     S2(n - 2, r)
-            E(n, 0)
-            S1(n, 2)
-            E(n, 1)
-            S1(n, 3)
+            E(n, 0, 0, DS)
+            S1full(n, 2)
+            E(n, 1, 0, DS)
+            S1full(n, 3)
             if n + 2 < NCH:
-                T(n + 2)
-            if n == last:
-                GQ(n - 1, 0, DS)
-            E(n, 2)
-            E(n, 3)
+                T(n + 2, 0)
+                T(n + 2, 1)
+            E(n, 2, 0, DS)
+            E(n, 3, 0, DS)
             if n == CH + 1:
                 for r in range(PACK):
-                    O(0, r, "ssss"[r])
-            if n < last:
-                GR(n, "s", 0, DS)
-                HQ(n + 1)
-            if 1 <= n < last:
+                    O(0, r, "s")
+            if n + 2 < NCH:
+                HC(n + 2, 0, "s")
+            GR(n, "s", 0, DS)
+            HQ(n + 1, 0, KP)
+            if n == 0:
+                PR(1, "v", PG1, DM)
+            if n >= 1:
                 GQ(n - 1, 0, DS)
-            if n < last:
-                PQ(n)
+            PQ(n)
             if n == last - 1:
                 PQ(last)
             if n + 2 < NCH:
-                HC(n + 2, ["s", "s"])
-                PRall(n + 2)
+                HC(n + 2, 1, "s")
+                PR(n + 2, "g", 0, PG)
+                PR(n + 2, "s", PG, DM)
 
+        S1pair(last, 0, 0)
+        S1pair(last, 2, 0)
+        for r in range(PACK):
+            S2(last - 2, r)
+        E(last, 0, 0, HALF)
+        E(last, 1, 0, HALF)
+        S1pair(last, 0, HALF)
+        E(last, 2, 0, HALF)
+        E(last, 3, 0, HALF)
+        S1pair(last, 2, HALF)
+        GR(last, "s", 0, HALF)
+        GQ(last - 1, 0, DS)
         for r in range(PACK):
             S2(last - 1, r)
-        for r in range(PACK):
-            GR(last, "vsvs"[r], P * r, P * r + P)
-        for r in range(PACK):
-            GQ(last, P * r, P * r + P)
-            S2(last, r)
-        for r in range(PACK):
-            O(1, r, "sv"[r % 2])
+        E(last, 0, HALF, DS)
+        E(last, 1, HALF, DS)
+        GQ(last, 0, HALF)
+        S2(last, 0)
+        S2(last, 1)
+        E(last, 2, HALF, DS)
+        E(last, 3, HALF, DS)
+        GR(last, "s", HALF + P, DS)
+        GR(last, "v", HALF, HALF + P)
+        GQ(last, HALF + P, DS)
+        S2(last, 3)
+        O(1, 0, "s")
+        GQ(last, HALF, HALF + P)
+        S2(last, 2)
+        O(1, 1, "s")
+        O(1, 3, "v")
+        O(1, 2, "s")

@@ -40,9 +40,7 @@ def tile_attractorstate_v2_kernel(tc, hidden_states, positional_encodings, W, b,
         work2 = ctx.enter_context(tc.tile_pool(name="work2", bufs=2))
         work3 = ctx.enter_context(tc.tile_pool(name="work3", bufs=3))
         work4 = ctx.enter_context(tc.tile_pool(name="work4", bufs=4))
-        tpool = ctx.enter_context(tc.psum_pool(name="tpool", bufs=2))
-        spool = ctx.enter_context(tc.psum_pool(name="spool", bufs=2))
-        apool = ctx.enter_context(tc.psum_pool(name="apool", bufs=1))
+        psum = ctx.enter_context(tc.psum_pool(name="psum", bufs=1))
         ctx.enter_context(tc.manual_schedule())
 
         brow = res.tile([P, DS], BF16, name="brow")
@@ -91,7 +89,7 @@ def tile_attractorstate_v2_kernel(tc, hidden_states, positional_encodings, W, b,
         nc.scalar.activation(out=wpc[:], in_=idxf[:], func=ACT.Exp, scale=math.pi / SEQ)
         ej = [math.exp(j * math.pi / SEQ) for j in range(PACK)]
 
-        psb = spool.tile([P, DS], F32, name="ps1")
+        psb = psum.tile([P, DS], F32, name="bank0")
         nc.tensor.matmul(out=psb[:], lhsT=ones[:], rhs=brow[:], start=True, stop=True)
         be = res.tile([P, PACK, DS], F32, name="be")
         nc.vector.tensor_copy(out=be[:, 0, :], in_=psb[:])
@@ -101,8 +99,8 @@ def tile_attractorstate_v2_kernel(tc, hidden_states, positional_encodings, W, b,
 
         st = {}
 
-        def transpose_half(key, words):
-            tp = tpool.tile([P, 2, 2, P], F32, name="tp")
+        def transpose_half(key, words, bank):
+            tp = psum.tile([P, 2, 2, P], F32, name=bank)
             for a in range(2):
                 for u in range(2):
                     col = 2 * P * a + P * u
@@ -120,8 +118,8 @@ def tile_attractorstate_v2_kernel(tc, hidden_states, positional_encodings, W, b,
         def quantise(grp_flat, codes, scales):
             nc.vector.quantize_mx(out=codes.bitcast(FP8X4), scales=scales, in_=grp_flat)
 
-        def T(n, h):
-            transpose_half((n, h), h_half[n, h])
+        def T(n, h, bank):
+            transpose_half((n, h), h_half[n, h], bank)
 
         def HC(n, h, eng):
             if h == 0:
@@ -143,20 +141,20 @@ def tile_attractorstate_v2_kernel(tc, hidden_states, positional_encodings, W, b,
                                 rhs=wq[:, lo:hi].bitcast(FP8X4), rhs_scale=ws[:, lo:hi], start=True, stop=True)
 
         def S1full(n, j):
-            ps = spool.tile([P, DS], F32, name="ps1")
+            ps = psum.tile([P, DS], F32, name="bank%d" % j)
             S1(n, j, ps[:], 0, DS)
-            st["ps", n, j] = ps[:]
+            st["ps", n, j, 0] = ps[:]
 
-        def S1pair(n, j, lo):
-            ps = spool.tile([P, DS], F32, name="ps1")
+        def S1pair(n, j, lo, bank):
+            ps = psum.tile([P, DS], F32, name=bank)
             for e in range(2):
                 S1(n, j + e, ps[:, HALF * e:HALF * e + HALF], lo, lo + HALF)
-                st["ps", n, j + e] = ps[:, HALF * e:HALF * e + HALF]
+                st["ps", n, j + e, lo] = ps[:, HALF * e:HALF * e + HALF]
 
         def E(n, j, lo, hi):
             if ("glin", n) not in st:
                 st["glin", n] = work3.tile([P, PACK, DS], F32, name="glin")
-            nc.vector.scalar_tensor_tensor(out=st["glin", n][:, j, lo:hi], in0=st["ps", n, j],
+            nc.vector.scalar_tensor_tensor(out=st["glin", n][:, j, lo:hi], in0=st["ps", n, j, lo],
                                            scalar=ej[j], in1=be[:, j, lo:hi], op0=ALU.mult, op1=ALU.add)
 
         def views(dst, src, lo, hi):
@@ -207,7 +205,7 @@ def tile_attractorstate_v2_kernel(tc, hidden_states, positional_encodings, W, b,
             gq, gs = st["gq", n]
             pq, pscale = st["pq", n]
             if c == 0:
-                st["acc", n // CH, r] = apool.tile([P, DM], F32, name="acc%d" % r)
+                st["acc", n // CH, r] = psum.tile([P, DM], F32, name="acc%d" % r)
             nc.tensor.matmul_mx(out=st["acc", n // CH, r][:],
                                 lhsT=gq[:, P * r:P * r + P].bitcast(FP8X4),
                                 lhsT_scale=gs[:, P * r:P * r + P],
@@ -226,11 +224,11 @@ def tile_attractorstate_v2_kernel(tc, hidden_states, positional_encodings, W, b,
         wq = res.tile([P, DS], U32, name="wq", align_bytes=64)
         ws = res.tile([P, DS], U8, name="ws", align_bytes=64)
         for h in range(2):
-            transpose_half(("w", h), w_half[h])
+            transpose_half(("w", h), w_half[h], "acc%d" % h)
         for h in range(2):
             copy_half(("w", h), wgrp, h, "s")
-        T(0, 0)
-        T(0, 1)
+        T(0, 0, "acc2")
+        T(0, 1, "acc3")
         quantise(wgrp[:], wq[:], ws[:])
         HC(0, 0, "s")
         HC(0, 1, "s")
@@ -239,60 +237,56 @@ def tile_attractorstate_v2_kernel(tc, hidden_states, positional_encodings, W, b,
         make_be(2)
         HQ(0, HALF, KP)
         make_be(3)
-        T(1, 0)
-        T(1, 1)
+        T(1, 0, "acc0")
+        T(1, 1, "acc1")
+        for j in range(PACK):
+            S1full(0, j)
         HC(1, 0, "s")
         HC(1, 1, "s")
-        S1full(0, 0)
-        S1full(0, 1)
         PR(0, "s", 0, DM)
         PR(1, "g", 0, PG1)
 
         for n in range(last):
-            if n > 0:
-                S1full(n, 0)
-                S1full(n, 1)
-            if n >= 2:
-                for r in range(PACK):
-                    S2(n - 2, r)
             E(n, 0, 0, DS)
-            S1full(n, 2)
             E(n, 1, 0, DS)
-            S1full(n, 3)
-            if n + 2 < NCH:
-                T(n + 2, 0)
-                T(n + 2, 1)
             E(n, 2, 0, DS)
+            if n + 2 < NCH:
+                T(n + 2, 0, "bank2")
             E(n, 3, 0, DS)
+            if n + 2 < NCH:
+                T(n + 2, 1, "bank3")
+                HC(n + 2, 0, "s")
+                HC(n + 2, 1, "s")
             if n == CH + 1:
                 for r in range(PACK):
                     O(0, r, "s")
-            if n + 2 < NCH:
-                HC(n + 2, 0, "s")
             GR(n, "s", 0, DS)
             HQ(n + 1, 0, KP)
+            if n + 1 < last:
+                for j in range(PACK):
+                    S1full(n + 1, j)
             if n == 0:
                 PR(1, "v", PG1, DM)
             if n >= 1:
                 GQ(n - 1, 0, DS)
+            if 1 <= n < last - 1:
+                for r in range(PACK):
+                    S2(n - 1, r)
             PQ(n)
             if n == last - 1:
                 PQ(last)
             if n + 2 < NCH:
-                HC(n + 2, 1, "s")
                 PR(n + 2, "g", 0, PG)
                 PR(n + 2, "s", PG, DM)
 
-        S1pair(last, 0, 0)
-        S1pair(last, 2, 0)
+        S1pair(last, 0, 0, "bank0")
+        S1pair(last, 2, 0, "bank1")
+        S1pair(last, 0, HALF, "bank2")
+        S1pair(last, 2, HALF, "bank3")
         for r in range(PACK):
             S2(last - 2, r)
-        E(last, 0, 0, HALF)
-        E(last, 1, 0, HALF)
-        S1pair(last, 0, HALF)
-        E(last, 2, 0, HALF)
-        E(last, 3, 0, HALF)
-        S1pair(last, 2, HALF)
+        for j in range(PACK):
+            E(last, j, 0, HALF)
         GR(last, "s", 0, HALF)
         GQ(last - 1, 0, DS)
         for r in range(PACK):

@@ -47,7 +47,7 @@ def tile_attractorstate_v2_kernel(tc, hidden_states, positional_encodings, W, b,
         nc.vector.memset(brow[:], 0.0)
         ones = res.tile([P, P], BF16, name="ones")
         nc.vector.memset(ones[:], 1.0)
-        nc.sync.dma_start(out=brow[0:1, :], in_=b.unsqueeze(0))
+        nc.scalar.dma_start(out=brow[0:1, :], in_=b.unsqueeze(0))
         w_half = []
         for h in range(2):
             wt = res.tile([P, 2 * DM], BF16, name="w_half%d" % h)

@@ -47,7 +47,8 @@ def tile_attractorstate_v2_kernel(tc, hidden_states, positional_encodings, W, b,
         nc.vector.memset(brow[:], 0.0)
         ones = res.tile([P, P], BF16, name="ones")
         nc.vector.memset(ones[:], 1.0)
-        nc.scalar.dma_start(out=brow[0:1, :], in_=b.unsqueeze(0))
+        bstage = res.tile([1, DS], BF16, name="bstage")
+        nc.sync.dma_start(out=bstage[:], in_=b.unsqueeze(0))
         w_half = []
         for h in range(2):
             wt = res.tile([P, 2 * DM], BF16, name="w_half%d" % h)
@@ -79,16 +80,17 @@ def tile_attractorstate_v2_kernel(tc, hidden_states, positional_encodings, W, b,
             load_h(n, 1)
             load_p(n)
 
-        ident = res.tile([P, P], F32, name="ident")
-        masks.make_identity(nc, ident[:])
         idx = res.tile([P, CH], I32, name="idx")
         nc.gpsimd.iota(idx[:], pattern=[[KP, CH]], base=1 - SEQ, channel_multiplier=PACK)
+        ident = res.tile([P, P], F32, name="ident")
+        masks.make_identity(nc, ident[:])
         idxf = res.tile([P, CH], F32, name="idxf")
         nc.vector.tensor_copy(out=idxf[:], in_=idx[:])
         wpc = res.tile([P, CH], F32, name="wpc")
         nc.scalar.activation(out=wpc[:], in_=idxf[:], func=ACT.Exp, scale=math.pi / SEQ)
         ej = [math.exp(j * math.pi / SEQ) for j in range(PACK)]
 
+        nc.vector.tensor_copy(out=brow[0:1, :], in_=bstage[:])
         psb = psum.tile([P, DS], F32, name="bank0")
         nc.tensor.matmul(out=psb[:], lhsT=ones[:], rhs=brow[:], start=True, stop=True)
         be = res.tile([P, PACK, DS], F32, name="be")
@@ -223,6 +225,8 @@ def tile_attractorstate_v2_kernel(tc, hidden_states, positional_encodings, W, b,
         wgrp = res.tile([P, PACK * KP], BF16, name="wgrp", align_bytes=64)
         wq = res.tile([P, DS], U32, name="wq", align_bytes=64)
         ws = res.tile([P, DS], U8, name="ws", align_bytes=64)
+        for j in range(1, PACK):
+            make_be(j)
         for h in range(2):
             transpose_half(("w", h), w_half[h], "acc%d" % h)
         for h in range(2):
@@ -232,11 +236,8 @@ def tile_attractorstate_v2_kernel(tc, hidden_states, positional_encodings, W, b,
         quantise(wgrp[:], wq[:], ws[:])
         HC(0, 0, "s")
         HC(0, 1, "s")
-        make_be(1)
         HQ(0, 0, HALF)
-        make_be(2)
         HQ(0, HALF, KP)
-        make_be(3)
         T(1, 0, "acc0")
         T(1, 1, "acc1")
         for j in range(PACK):

@@ -258,7 +258,7 @@ def tile_attractorstate_v2_kernel(tc, hidden_states, positional_encodings, W, b,
                 T(n + 2, 1, "bank3")
                 HC(n + 2, 0, "s")
                 HC(n + 2, 1, "s")
-            if n == CH + 1:
+            if n == last - 1:
                 for r in range(PACK):
                     O(0, r, "s")
             GR(n, "s", 0, DS)
@@ -270,13 +270,15 @@ def tile_attractorstate_v2_kernel(tc, hidden_states, positional_encodings, W, b,
                 PR(1, "v", PG1, DM)
             if n >= 1:
                 GQ(n - 1, 0, DS)
-            if 1 <= n < last - 1:
+            if n == last - 1:
+                break
+            if 1 <= n <= CH:
                 for r in range(PACK):
                     S2(n - 1, r)
             PQ(n)
-            if n == last - 1:
-                PQ(last)
-            if n + 2 < NCH:
+            if n + 2 == last:
+                PR(last, "g", 0, DM)
+            elif n + 2 < NCH:
                 PR(n + 2, "g", 0, PG)
                 PR(n + 2, "s", PG, DM)
 
@@ -284,28 +286,27 @@ def tile_attractorstate_v2_kernel(tc, hidden_states, positional_encodings, W, b,
         S1pair(last, 2, 0, "bank1")
         S1pair(last, 0, HALF, "bank2")
         S1pair(last, 2, HALF, "bank3")
-        for r in range(PACK):
-            S2(last - 2, r)
+        for n in (last - 3, last - 2):
+            for r in range(PACK):
+                S2(n, r)
         for j in range(PACK):
             E(last, j, 0, HALF)
         GR(last, "s", 0, HALF)
+        for j in range(PACK):
+            E(last, j, HALF, DS)
+        GR(last, "s", HALF, DS)
+        PQ(last - 1)
         GQ(last - 1, 0, DS)
         for r in range(PACK):
             S2(last - 1, r)
-        E(last, 0, HALF, DS)
-        E(last, 1, HALF, DS)
+        PQ(last)
         GQ(last, 0, HALF)
         S2(last, 0)
         S2(last, 1)
-        E(last, 2, HALF, DS)
-        E(last, 3, HALF, DS)
-        GR(last, "s", HALF + P, DS)
-        GR(last, "v", HALF, HALF + P)
-        GQ(last, HALF + P, DS)
+        GQ(last, HALF, DS)
+        S2(last, 2)
         S2(last, 3)
         O(1, 0, "s")
-        GQ(last, HALF, HALF + P)
-        S2(last, 2)
-        O(1, 1, "s")
-        O(1, 3, "v")
+        O(1, 1, "v")
         O(1, 2, "s")
+        O(1, 3, "v")

@@ -26,7 +26,6 @@ HALF = DS // 2
 FLOPS = 2 * BATCH * SEQ * DM * DS + 2 * BATCH * DS * DM * SEQ
 
 PG = 384
-PG1 = 256
 
 
 def tile_attractorstate_v2_kernel(tc, hidden_states, positional_encodings, W, b, out):
@@ -73,12 +72,10 @@ def tile_attractorstate_v2_kernel(tc, hidden_states, positional_encodings, W, b,
             p_sb[n] = pt
 
         load_h(0, 2)
-        load_h(1, 1)
-        load_p(0)
-        load_p(1)
-        for n in range(2, NCH):
+        for n in range(1, NCH):
             load_h(n, 1)
-            load_p(n)
+            load_p(n - 1)
+        load_p(last)
 
         idx = res.tile([P, CH], I32, name="idx")
         nc.gpsimd.iota(idx[:], pattern=[[KP, CH]], base=1 - SEQ, channel_multiplier=PACK)
@@ -96,8 +93,11 @@ def tile_attractorstate_v2_kernel(tc, hidden_states, positional_encodings, W, b,
         be = res.tile([P, PACK, DS], F32, name="be")
         nc.vector.tensor_copy(out=be[:, 0, :], in_=psb[:])
 
-        def make_be(j):
-            nc.vector.tensor_scalar(out=be[:, j, :], in0=be[:, 0, :], scalar1=ej[j], scalar2=None, op0=ALU.mult)
+        def make_be(j, eng):
+            if eng == "v":
+                nc.vector.tensor_scalar(out=be[:, j, :], in0=be[:, 0, :], scalar1=ej[j], scalar2=None, op0=ALU.mult)
+            else:
+                nc.scalar.activation(out=be[:, j, :], in_=be[:, 0, :], func=ACT.Copy, scale=ej[j])
 
         st = {}
 
@@ -225,80 +225,84 @@ def tile_attractorstate_v2_kernel(tc, hidden_states, positional_encodings, W, b,
         wgrp = res.tile([P, PACK * KP], BF16, name="wgrp", align_bytes=64)
         wq = res.tile([P, DS], U32, name="wq", align_bytes=64)
         ws = res.tile([P, DS], U8, name="ws", align_bytes=64)
-        for j in range(1, PACK):
-            make_be(j)
+        make_be(1, "v")
         for h in range(2):
             transpose_half(("w", h), w_half[h], "acc%d" % h)
-        for h in range(2):
-            copy_half(("w", h), wgrp, h, "s")
         T(0, 0, "acc2")
         T(0, 1, "acc3")
+        copy_half(("w", 0), wgrp, 0, "s")
+        copy_half(("w", 1), wgrp, 1, "v")
         quantise(wgrp[:], wq[:], ws[:])
         HC(0, 0, "s")
         HC(0, 1, "s")
         HQ(0, 0, HALF)
         HQ(0, HALF, KP)
+        for j in range(2, PACK):
+            make_be(j, "s")
+        S1full(0, 0)
+        S1full(0, 1)
         T(1, 0, "acc0")
+        S1full(0, 2)
         T(1, 1, "acc1")
-        for j in range(PACK):
-            S1full(0, j)
+        S1full(0, 3)
         HC(1, 0, "s")
         HC(1, 1, "s")
-        PR(0, "s", 0, DM)
-        PR(1, "g", 0, PG1)
+        PR(0, "g", 0, DM)
 
         for n in range(last):
+            if n == last - 1:
+                PR(n, "g", 0, DM)
+                O(0, 0, "s")
+                O(0, 1, "s")
+                O(0, 2, "s")
+            elif n > 0:
+                PR(n, "g", 0, PG)
+                PR(n, "s", PG, DM)
             E(n, 0, 0, DS)
             E(n, 1, 0, DS)
             E(n, 2, 0, DS)
-            if n + 2 < NCH:
+            if 0 < n and n + 2 < NCH:
                 T(n + 2, 0, "bank2")
             E(n, 3, 0, DS)
-            if n + 2 < NCH:
+            if 0 < n and n + 2 < NCH:
                 T(n + 2, 1, "bank3")
                 HC(n + 2, 0, "s")
                 HC(n + 2, 1, "s")
-            if n == last - 1:
-                for r in range(PACK):
-                    O(0, r, "s")
             GR(n, "s", 0, DS)
+            if n == 0:
+                T(2, 0, "acc2")
+                T(2, 1, "acc3")
+                HC(2, 0, "s")
+                HC(2, 1, "s")
             HQ(n + 1, 0, KP)
-            if n + 1 < last:
+            if n == last - 1:
+                S1pair(last, 0, 0, "bank0")
+                S1pair(last, 2, 0, "bank1")
+                S1pair(last, 0, HALF, "bank2")
+                S1pair(last, 2, HALF, "bank3")
+            else:
                 for j in range(PACK):
                     S1full(n + 1, j)
-            if n == 0:
-                PR(1, "v", PG1, DM)
             if n >= 1:
                 GQ(n - 1, 0, DS)
             if n == last - 1:
-                break
-            if 1 <= n <= CH:
-                for r in range(PACK):
-                    S2(n - 1, r)
+                O(0, 3, "v")
+            if 1 <= n <= CH or n == last - 1:
+                for k in range(n - 1 if n <= CH else n - 2, n):
+                    for r in range(PACK):
+                        S2(k, r)
             PQ(n)
-            if n + 2 == last:
-                PR(last, "g", 0, DM)
-            elif n + 2 < NCH:
-                PR(n + 2, "g", 0, PG)
-                PR(n + 2, "s", PG, DM)
 
-        S1pair(last, 0, 0, "bank0")
-        S1pair(last, 2, 0, "bank1")
-        S1pair(last, 0, HALF, "bank2")
-        S1pair(last, 2, HALF, "bank3")
-        for n in (last - 3, last - 2):
-            for r in range(PACK):
-                S2(n, r)
+        PR(last, "g", 0, DM)
         for j in range(PACK):
             E(last, j, 0, HALF)
         GR(last, "s", 0, HALF)
-        for j in range(PACK):
-            E(last, j, HALF, DS)
-        GR(last, "s", HALF, DS)
-        PQ(last - 1)
         GQ(last - 1, 0, DS)
         for r in range(PACK):
             S2(last - 1, r)
+        for j in range(PACK):
+            E(last, j, HALF, DS)
+        GR(last, "s", HALF, DS)
         PQ(last)
         GQ(last, 0, HALF)
         S2(last, 0)

@@ -38,6 +38,7 @@ def tile_attractorstate_v2_kernel(tc, hidden_states, positional_encodings, W, b,
         res = ctx.enter_context(tc.tile_pool(name="res", bufs=1))
         work2 = ctx.enter_context(tc.tile_pool(name="work2", bufs=2))
         work3 = ctx.enter_context(tc.tile_pool(name="work3", bufs=3))
+        work1 = ctx.enter_context(tc.tile_pool(name="work1", bufs=1))
         work4 = ctx.enter_context(tc.tile_pool(name="work4", bufs=4))
         psum = ctx.enter_context(tc.psum_pool(name="psum", bufs=1))
         ctx.enter_context(tc.manual_schedule())
@@ -88,13 +89,12 @@ def tile_attractorstate_v2_kernel(tc, hidden_states, positional_encodings, W, b,
         ej = [math.exp(j * math.pi / SEQ) for j in range(PACK)]
 
         nc.vector.tensor_copy(out=brow[0:1, :], in_=bstage[:])
-        psb = psum.tile([P, DS], F32, name="bank0")
-        nc.tensor.matmul(out=psb[:], lhsT=ones[:], rhs=brow[:], start=True, stop=True)
         be = res.tile([P, PACK, DS], F32, name="be")
-        nc.vector.tensor_copy(out=be[:, 0, :], in_=psb[:])
 
         def make_be(j, eng):
-            if eng == "v":
+            if j == 0:
+                nc.vector.tensor_copy(out=be[:, 0, :], in_=psb[:])
+            elif eng == "v":
                 nc.vector.tensor_scalar(out=be[:, j, :], in0=be[:, 0, :], scalar1=ej[j], scalar2=None, op0=ALU.mult)
             else:
                 nc.scalar.activation(out=be[:, j, :], in_=be[:, 0, :], func=ACT.Copy, scale=ej[j])
@@ -184,7 +184,7 @@ def tile_attractorstate_v2_kernel(tc, hidden_states, positional_encodings, W, b,
 
         def PR(n, eng, lo, hi):
             if ("pgrp", n) not in st:
-                st["pgrp", n] = work2.tile([P, DM, PACK], BF16, name="pgrp", align_bytes=64)
+                st["pgrp", n] = work1.tile([P, DM, PACK], BF16, name="pgrp", align_bytes=64)
             if eng == "g":
                 nc.gpsimd.tensor_scalar(out=st["pgrp", n][:, lo:hi, :],
                                         in0=p_sb[n][:, :, lo:hi].rearrange("p t c -> p c t"),
@@ -225,20 +225,23 @@ def tile_attractorstate_v2_kernel(tc, hidden_states, positional_encodings, W, b,
         wgrp = res.tile([P, PACK * KP], BF16, name="wgrp", align_bytes=64)
         wq = res.tile([P, DS], U32, name="wq", align_bytes=64)
         ws = res.tile([P, DS], U8, name="ws", align_bytes=64)
-        make_be(1, "v")
         for h in range(2):
             transpose_half(("w", h), w_half[h], "acc%d" % h)
+        psb = psum.tile([P, DS], F32, name="bank0")
+        nc.tensor.matmul(out=psb[:], lhsT=ones[:], rhs=brow[:], start=True, stop=True)
         T(0, 0, "acc2")
         T(0, 1, "acc3")
-        copy_half(("w", 0), wgrp, 0, "s")
-        copy_half(("w", 1), wgrp, 1, "v")
+        copy_half(("w", 0), wgrp, 0, "v")
+        copy_half(("w", 1), wgrp, 1, "s")
+        make_be(0, "v")
         quantise(wgrp[:], wq[:], ws[:])
         HC(0, 0, "s")
         HC(0, 1, "s")
         HQ(0, 0, HALF)
+        make_be(1, "v")
         HQ(0, HALF, KP)
-        for j in range(2, PACK):
-            make_be(j, "s")
+        make_be(2, "s")
+        make_be(3, "s")
         S1full(0, 0)
         S1full(0, 1)
         T(1, 0, "acc0")
@@ -247,17 +250,14 @@ def tile_attractorstate_v2_kernel(tc, hidden_states, positional_encodings, W, b,
         S1full(0, 3)
         HC(1, 0, "s")
         HC(1, 1, "s")
-        PR(0, "g", 0, DM)
 
         for n in range(last):
+            PR(n, "g", 0, PG)
+            PR(n, "s", PG, DM)
             if n == last - 1:
-                PR(n, "g", 0, DM)
                 O(0, 0, "s")
                 O(0, 1, "s")
                 O(0, 2, "s")
-            elif n > 0:
-                PR(n, "g", 0, PG)
-                PR(n, "s", PG, DM)
             E(n, 0, 0, DS)
             E(n, 1, 0, DS)
             E(n, 2, 0, DS)
@@ -293,16 +293,17 @@ def tile_attractorstate_v2_kernel(tc, hidden_states, positional_encodings, W, b,
                         S2(k, r)
             PQ(n)
 
-        PR(last, "g", 0, DM)
+        PR(last, "g", 0, PG)
         for j in range(PACK):
             E(last, j, 0, HALF)
         GR(last, "s", 0, HALF)
-        GQ(last - 1, 0, DS)
-        for r in range(PACK):
-            S2(last - 1, r)
+        PR(last, "s", PG, DM)
         for j in range(PACK):
             E(last, j, HALF, DS)
         GR(last, "s", HALF, DS)
+        GQ(last - 1, 0, DS)
+        for r in range(PACK):
+            S2(last - 1, r)
         PQ(last)
         GQ(last, 0, HALF)
         S2(last, 0)

@@ -43,10 +43,12 @@ def tile_attractorstate_v2_kernel(tc, hidden_states, positional_encodings, W, b,
         psum = ctx.enter_context(tc.psum_pool(name="psum", bufs=1))
         ctx.enter_context(tc.manual_schedule())
 
-        brow = res.tile([P, DS], BF16, name="brow")
-        nc.vector.memset(brow[:], 0.0)
+        zeros = res.tile([P, DS], BF16, name="zeros")
+        nc.vector.memset(zeros[:], 0.0)
         ones = res.tile([P, P], BF16, name="ones")
         nc.vector.memset(ones[:], 1.0)
+        brow = res.tile([P, DS], BF16, name="brow")
+        nc.vector.memset(brow[:], 0.0)
         bstage = res.tile([1, DS], BF16, name="bstage")
         nc.sync.dma_start(out=bstage[:], in_=b.unsqueeze(0))
         w_half = []
@@ -88,16 +90,21 @@ def tile_attractorstate_v2_kernel(tc, hidden_states, positional_encodings, W, b,
         nc.scalar.activation(out=wpc[:], in_=idxf[:], func=ACT.Exp, scale=math.pi / SEQ)
         ej = [math.exp(j * math.pi / SEQ) for j in range(PACK)]
 
+        def keep_busy(bank, width=DS):
+            spare = psum.tile([P, DS], F32, name=bank)
+            nc.tensor.matmul(out=spare[:, 0:width], lhsT=zeros[:, 0:P], rhs=zeros[:, 0:width], start=True, stop=True)
+
         nc.vector.tensor_copy(out=brow[0:1, :], in_=bstage[:])
         be = res.tile([P, PACK, DS], F32, name="be")
 
         def make_be(j, eng):
-            if j == 0:
+            src, factor = (psb[:], 1.0) if j == 0 else (be[:, 0, :], ej[j])
+            if eng == "v" and j == 0:
                 nc.vector.tensor_copy(out=be[:, 0, :], in_=psb[:])
             elif eng == "v":
-                nc.vector.tensor_scalar(out=be[:, j, :], in0=be[:, 0, :], scalar1=ej[j], scalar2=None, op0=ALU.mult)
+                nc.vector.tensor_scalar(out=be[:, j, :], in0=src, scalar1=factor, scalar2=None, op0=ALU.mult)
             else:
-                nc.scalar.activation(out=be[:, j, :], in_=be[:, 0, :], func=ACT.Copy, scale=ej[j])
+                nc.scalar.activation(out=be[:, j, :], in_=src, func=ACT.Copy, scale=factor)
 
         st = {}
 
@@ -225,26 +232,30 @@ def tile_attractorstate_v2_kernel(tc, hidden_states, positional_encodings, W, b,
         wgrp = res.tile([P, PACK * KP], BF16, name="wgrp", align_bytes=64)
         wq = res.tile([P, DS], U32, name="wq", align_bytes=64)
         ws = res.tile([P, DS], U8, name="ws", align_bytes=64)
-        for h in range(2):
-            transpose_half(("w", h), w_half[h], "acc%d" % h)
+        for k in range(5):
+            keep_busy("bank%d" % (1 + k % 3))
         psb = psum.tile([P, DS], F32, name="bank0")
         nc.tensor.matmul(out=psb[:], lhsT=ones[:], rhs=brow[:], start=True, stop=True)
-        T(0, 0, "acc2")
-        T(0, 1, "acc3")
+        make_be(0, "s")
+        transpose_half(("w", 0), w_half[0], "acc0")
+        transpose_half(("w", 1), w_half[1], "acc1")
         copy_half(("w", 0), wgrp, 0, "v")
         copy_half(("w", 1), wgrp, 1, "s")
-        make_be(0, "v")
+        make_be(1, "v")
+        make_be(2, "v")
+        keep_busy("bank2")
+        T(0, 0, "acc2")
+        T(0, 1, "acc3")
+        keep_busy("bank3")
         quantise(wgrp[:], wq[:], ws[:])
         HC(0, 0, "s")
         HC(0, 1, "s")
         HQ(0, 0, HALF)
-        make_be(1, "v")
         HQ(0, HALF, KP)
-        make_be(2, "s")
         make_be(3, "s")
+        T(1, 0, "acc0")
         S1full(0, 0)
         S1full(0, 1)
-        T(1, 0, "acc0")
         S1full(0, 2)
         T(1, 1, "acc1")
         S1full(0, 3)
@@ -258,11 +269,13 @@ def tile_attractorstate_v2_kernel(tc, hidden_states, positional_encodings, W, b,
                 O(0, 0, "s")
                 O(0, 1, "s")
                 O(0, 2, "s")
+                O(0, 3, "s")
             E(n, 0, 0, DS)
             E(n, 1, 0, DS)
             E(n, 2, 0, DS)
             if 0 < n and n + 2 < NCH:
                 T(n + 2, 0, "bank2")
+            keep_busy("bank1")
             E(n, 3, 0, DS)
             if 0 < n and n + 2 < NCH:
                 T(n + 2, 1, "bank3")
@@ -286,30 +299,34 @@ def tile_attractorstate_v2_kernel(tc, hidden_states, positional_encodings, W, b,
             if n >= 1:
                 GQ(n - 1, 0, DS)
             if n == last - 1:
-                O(0, 3, "v")
+                pass
             if 1 <= n <= CH or n == last - 1:
                 for k in range(n - 1 if n <= CH else n - 2, n):
                     for r in range(PACK):
                         S2(k, r)
             PQ(n)
 
-        PR(last, "g", 0, PG)
+        PR(last, "g", 0, 448)
         for j in range(PACK):
             E(last, j, 0, HALF)
         GR(last, "s", 0, HALF)
-        PR(last, "s", PG, DM)
         for j in range(PACK):
             E(last, j, HALF, DS)
-        GR(last, "s", HALF, DS)
+        GR(last, "s", HALF, HALF + P)
+        GR(last, "s", HALF + P, DS)
+        PR(last, "v", 448, DM)
         GQ(last - 1, 0, DS)
-        for r in range(PACK):
-            S2(last - 1, r)
+        S2(last - 1, 0)
+        S2(last - 1, 1)
         PQ(last)
         GQ(last, 0, HALF)
         S2(last, 0)
         S2(last, 1)
-        GQ(last, HALF, DS)
+        S2(last - 1, 2)
+        S2(last - 1, 3)
+        GQ(last, HALF, HALF + P)
         S2(last, 2)
+        GQ(last, HALF + P, DS)
         S2(last, 3)
         O(1, 0, "s")
         O(1, 1, "v")

@@ -43,12 +43,14 @@ def tile_attractorstate_v2_kernel(tc, hidden_states, positional_encodings, W, b,
         psum = ctx.enter_context(tc.psum_pool(name="psum", bufs=1))
         ctx.enter_context(tc.manual_schedule())
 
-        zeros = res.tile([P, DS], BF16, name="zeros")
-        nc.vector.memset(zeros[:], 0.0)
+        idle = res.tile([P, P], BF16, name="idle")
+        nc.vector.memset(idle[:], 0.0)
         ones = res.tile([P, P], BF16, name="ones")
         nc.vector.memset(ones[:], 1.0)
         brow = res.tile([P, DS], BF16, name="brow")
         nc.vector.memset(brow[:], 0.0)
+        zeros = res.tile([P, DS], BF16, name="zeros")
+        nc.vector.memset(zeros[:], 0.0)
         bstage = res.tile([1, DS], BF16, name="bstage")
         nc.sync.dma_start(out=bstage[:], in_=b.unsqueeze(0))
         w_half = []
@@ -232,8 +234,9 @@ def tile_attractorstate_v2_kernel(tc, hidden_states, positional_encodings, W, b,
         wgrp = res.tile([P, PACK * KP], BF16, name="wgrp", align_bytes=64)
         wq = res.tile([P, DS], U32, name="wq", align_bytes=64)
         ws = res.tile([P, DS], U8, name="ws", align_bytes=64)
-        for k in range(5):
-            keep_busy("bank%d" % (1 + k % 3))
+        for k in range(18):
+            spare = psum.tile([P, DS], F32, name="bank%d" % (1 + k % 3))
+            nc.tensor.matmul(out=spare[:, 0:P], lhsT=idle[:], rhs=idle[:], start=True, stop=True)
         psb = psum.tile([P, DS], F32, name="bank0")
         nc.tensor.matmul(out=psb[:], lhsT=ones[:], rhs=brow[:], start=True, stop=True)
         make_be(0, "s")

from contextlib import ExitStack
import math

import concourse.masks as masks
import concourse.mybir as mybir

F32 = mybir.dt.float32
BF16 = mybir.dt.bfloat16
U32 = mybir.dt.uint32
U8 = mybir.dt.uint8
I32 = mybir.dt.int32
FP8X4 = mybir.dt.float8_e4m3fn_x4
ALU = mybir.AluOpType
ACT = mybir.ActivationFunctionType

P = 128
PACK = 4
KP = P * PACK
BATCH = 2
SEQ = 2048
DM = 512
DS = 512
CH = SEQ // KP
NCH = BATCH * CH
HALF = DS // 2
FLOPS = 2 * BATCH * SEQ * DM * DS + 2 * BATCH * DS * DM * SEQ

PG = 384


def tile_attractorstate_v2_kernel(tc, hidden_states, positional_encodings, W, b, out):
    nc = tc.nc
    h_dram = hidden_states.flatten_outer_dims().rearrange("(n p j) d -> n p (j d)", p=P, j=PACK)
    p_dram = positional_encodings.flatten_outer_dims().rearrange("(n p j) m -> n p (j m)", p=P, j=PACK)
    last = NCH - 1

    with ExitStack() as ctx:
        res = ctx.enter_context(tc.tile_pool(name="res", bufs=1))
        work2 = ctx.enter_context(tc.tile_pool(name="work2", bufs=2))
        work3 = ctx.enter_context(tc.tile_pool(name="work3", bufs=3))
        work1 = ctx.enter_context(tc.tile_pool(name="work1", bufs=1))
        work4 = ctx.enter_context(tc.tile_pool(name="work4", bufs=4))
        psum = ctx.enter_context(tc.psum_pool(name="psum", bufs=1))
        ctx.enter_context(tc.manual_schedule())

        idle = res.tile([P, P], BF16, name="idle")
        nc.vector.memset(idle[:], 0.0)
        ones = res.tile([P, P], BF16, name="ones")
        nc.vector.memset(ones[:], 1.0)
        brow = res.tile([P, DS], BF16, name="brow")
        nc.vector.memset(brow[:], 0.0)
        zeros = res.tile([P, DS], BF16, name="zeros")
        nc.vector.memset(zeros[:], 0.0)
        bstage = res.tile([1, DS], BF16, name="bstage")
        nc.sync.dma_start(out=bstage[:], in_=b.unsqueeze(0))
        w_half = []
        for h in range(2):
            wt = res.tile([P, 2 * DM], BF16, name="w_half%d" % h)
            nc.sync.dma_start(out=wt[:].rearrange("p (r d) -> p r d", r=2),
                              in_=W[2 * P * h:2 * P * h + 2 * P, :].rearrange("(r p) d -> p r d", p=P))
            w_half.append(wt[:].bitcast(F32))
        h_half = {}
        p_sb = {}

        def load_h(n, pieces):
            width = PACK * DM // pieces
            for q in range(pieces):
                ht = res.tile([P, width], BF16, name="h_sb%d_%d" % (n, q))
                nc.sync.dma_start(out=ht[:], in_=h_dram[n][:, width * q:width * q + width])
                words = ht[:].bitcast(F32)
                for h in range(2 // pieces):
                    h_half[n, q * (2 // pieces) + h] = words[:, DM * h:DM * h + DM]

        def load_p(n):
            pt = res.tile([P, PACK, DM], BF16, name="p_sb%d" % n)
            nc.sync.dma_start(out=pt[:].rearrange("p j m -> p (j m)"), in_=p_dram[n])
            p_sb[n] = pt

        load_h(0, 2)
        for n in range(1, NCH):
            load_h(n, 1)
            load_p(n - 1)
        load_p(last)

        idx = res.tile([P, CH], I32, name="idx")
        nc.gpsimd.iota(idx[:], pattern=[[KP, CH]], base=1 - SEQ, channel_multiplier=PACK)
        ident = res.tile([P, P], F32, name="ident")
        masks.make_identity(nc, ident[:])
        idxf = res.tile([P, CH], F32, name="idxf")
        nc.vector.tensor_copy(out=idxf[:], in_=idx[:])
        wpc = res.tile([P, CH], F32, name="wpc")
        nc.scalar.activation(out=wpc[:], in_=idxf[:], func=ACT.Exp, scale=math.pi / SEQ)
        ej = [math.exp(j * math.pi / SEQ) for j in range(PACK)]

        def keep_busy(bank, width=DS):
            spare = psum.tile([P, DS], F32, name=bank)
            nc.tensor.matmul(out=spare[:, 0:width], lhsT=zeros[:, 0:P], rhs=zeros[:, 0:width], start=True, stop=True)

        nc.vector.tensor_copy(out=brow[0:1, :], in_=bstage[:])
        be = res.tile([P, PACK, DS], F32, name="be")

        def make_be(j, eng):
            src, factor = (psb[:], 1.0) if j == 0 else (be[:, 0, :], ej[j])
            if eng == "v" and j == 0:
                nc.vector.tensor_copy(out=be[:, 0, :], in_=psb[:])
            elif eng == "v":
                nc.vector.tensor_scalar(out=be[:, j, :], in0=src, scalar1=factor, scalar2=None, op0=ALU.mult)
            else:
                nc.scalar.activation(out=be[:, j, :], in_=src, func=ACT.Copy, scale=factor)

        st = {}

        def transpose_half(key, words, bank):
            tp = psum.tile([P, 2, 2, P], F32, name=bank)
            for a in range(2):
                for u in range(2):
                    col = 2 * P * a + P * u
                    nc.tensor.transpose(tp[:, a, u, :], words[:, col:col + P], ident[:])
            st["tp", key] = tp

        def copy_half(key, grp, h, eng):
            dst = grp[:].bitcast(F32)[:, DM * h:DM * h + DM].rearrange("q (a p u) -> q a p u", a=2, u=2)
            src = st["tp", key][:].rearrange("q a u p -> q a p u")
            if eng == "v":
                nc.vector.tensor_copy(out=dst, in_=src)
            else:
                nc.scalar.copy(out=dst, in_=src)

        def quantise(grp_flat, codes, scales):
            nc.vector.quantize_mx(out=codes.bitcast(FP8X4), scales=scales, in_=grp_flat)

        def T(n, h, bank):
            transpose_half((n, h), h_half[n, h], bank)

        def HC(n, h, eng):
            if h == 0:
                st["hgrp", n] = work2.tile([P, PACK * KP], BF16, name="hgrp", align_bytes=64)
            copy_half((n, h), st["hgrp", n], h, eng)

        def HQ(n, lo, hi):
            if ("hq", n) not in st:
                hq = work2.tile([P, KP], U32, name="hq", align_bytes=64)
                hs = work2.tile([P, KP], U8, name="hs", align_bytes=64)
                st["hq", n] = (hq, hs)
            hq, hs = st["hq", n]
            quantise(st["hgrp", n][:, PACK * lo:PACK * hi], hq[:, lo:hi], hs[:, lo:hi])

        def S1(n, j, ps, lo, hi):
            hq, hs = st["hq", n]
            nc.tensor.matmul_mx(out=ps, lhsT=hq[:, P * j:P * j + P].bitcast(FP8X4),
                                lhsT_scale=hs[:, P * j:P * j + P],
                                rhs=wq[:, lo:hi].bitcast(FP8X4), rhs_scale=ws[:, lo:hi], start=True, stop=True)

        def S1full(n, j):
            ps = psum.tile([P, DS], F32, name="bank%d" % j)
            S1(n, j, ps[:], 0, DS)
            st["ps", n, j, 0] = ps[:]

        def S1pair(n, j, lo, bank):
            ps = psum.tile([P, DS], F32, name=bank)
            for e in range(2):
                S1(n, j + e, ps[:, HALF * e:HALF * e + HALF], lo, lo + HALF)
                st["ps", n, j + e, lo] = ps[:, HALF * e:HALF * e + HALF]

        def E(n, j, lo, hi):
            if ("glin", n) not in st:
                st["glin", n] = work3.tile([P, PACK, DS], F32, name="glin")
            nc.vector.scalar_tensor_tensor(out=st["glin", n][:, j, lo:hi], in0=st["ps", n, j, lo],
                                           scalar=ej[j], in1=be[:, j, lo:hi], op0=ALU.mult, op1=ALU.add)

        def views(dst, src, lo, hi):
            d = dst[:, lo:hi, :].rearrange("p (c i) t -> p c t i", i=4)
            s = src[:, :, lo:hi].rearrange("p t (c i) -> p c t i", i=4)
            return d, s

        def GR(n, eng, lo, hi):
            if ("ggrp", n) not in st:
                st["ggrp", n] = work2.tile([P, DS, PACK], BF16, name="ggrp", align_bytes=64)
            d, s = views(st["ggrp", n], st["glin", n], lo, hi)
            c = n % CH
            if eng == "v":
                nc.vector.tensor_scalar(out=d, in0=s, scalar1=wpc[:, c:c + 1], scalar2=None, op0=ALU.mult)
            else:
                nc.scalar.activation(out=d, in_=s, func=ACT.Copy, scale=wpc[:, c:c + 1])

        def GQ(n, lo, hi):
            if ("gq", n) not in st:
                gq = work2.tile([P, DS], U32, name="gq", align_bytes=64)
                gs = work2.tile([P, DS], U8, name="gs", align_bytes=64)
                st["gq", n] = (gq, gs)
            gq, gs = st["gq", n]
            quantise(st["ggrp", n][:, lo:hi, :].rearrange("p s j -> p (s j)"), gq[:, lo:hi], gs[:, lo:hi])

        def PR(n, eng, lo, hi):
            if ("pgrp", n) not in st:
                st["pgrp", n] = work1.tile([P, DM, PACK], BF16, name="pgrp", align_bytes=64)
            if eng == "g":
                nc.gpsimd.tensor_scalar(out=st["pgrp", n][:, lo:hi, :],
                                        in0=p_sb[n][:, :, lo:hi].rearrange("p t c -> p c t"),
                                        scalar1=1.0, scalar2=0.0, op0=ALU.mult, op1=ALU.add)
                return
            d, s = views(st["pgrp", n], p_sb[n], lo, hi)
            if eng == "v":
                nc.vector.tensor_copy(out=d, in_=s)
            else:
                nc.scalar.copy(out=d, in_=s)

        def PQ(n):
            pq = work4.tile([P, DM], U32, name="pq", align_bytes=64)
            pscale = work4.tile([P, DM], U8, name="pscale", align_bytes=64)
            quantise(st["pgrp", n][:].rearrange("p m j -> p (m j)"), pq[:], pscale[:])
            st["pq", n] = (pq, pscale)

        def S2(n, r):
            c = n % CH
            gq, gs = st["gq", n]
            pq, pscale = st["pq", n]
            if c == 0:
                st["acc", n // CH, r] = psum.tile([P, DM], F32, name="acc%d" % r)
            nc.tensor.matmul_mx(out=st["acc", n // CH, r][:],
                                lhsT=gq[:, P * r:P * r + P].bitcast(FP8X4),
                                lhsT_scale=gs[:, P * r:P * r + P],
                                rhs=pq[:].bitcast(FP8X4), rhs_scale=pscale[:],
                                start=(c == 0), stop=(c == CH - 1))

        def O(i, r, eng):
            osb = work4.tile([P, DM], F32, name="osb")
            if eng == "s":
                nc.scalar.copy(out=osb[:], in_=st["acc", i, r][:])
            else:
                nc.vector.tensor_copy(out=osb[:], in_=st["acc", i, r][:])
            nc.sync.dma_start(out=out[i, P * r:P * r + P, :], in_=osb[:])

        wgrp = res.tile([P, PACK * KP], BF16, name="wgrp", align_bytes=64)
        wq = res.tile([P, DS], U32, name="wq", align_bytes=64)
        ws = res.tile([P, DS], U8, name="ws", align_bytes=64)
        for k in range(18):
            spare = psum.tile([P, DS], F32, name="bank%d" % (1 + k % 3))
            nc.tensor.matmul(out=spare[:, 0:P], lhsT=idle[:], rhs=idle[:], start=True, stop=True)
        psb = psum.tile([P, DS], F32, name="bank0")
        nc.tensor.matmul(out=psb[:], lhsT=ones[:], rhs=brow[:], start=True, stop=True)
        make_be(0, "s")
        transpose_half(("w", 0), w_half[0], "acc0")
        transpose_half(("w", 1), w_half[1], "acc1")
        copy_half(("w", 0), wgrp, 0, "v")
        copy_half(("w", 1), wgrp, 1, "s")
        make_be(1, "v")
        make_be(2, "v")
        keep_busy("bank2")
        T(0, 0, "acc2")
        T(0, 1, "acc3")
        keep_busy("bank3")
        quantise(wgrp[:], wq[:], ws[:])
        HC(0, 0, "s")
        HC(0, 1, "s")
        HQ(0, 0, HALF)
        HQ(0, HALF, KP)
        make_be(3, "s")
        T(1, 0, "acc0")
        S1full(0, 0)
        S1full(0, 1)
        S1full(0, 2)
        T(1, 1, "acc1")
        S1full(0, 3)
        HC(1, 0, "s")
        HC(1, 1, "s")

        for n in range(last):
            PR(n, "g", 0, PG)
            PR(n, "s", PG, DM)
            if n == last - 1:
                O(0, 0, "s")
                O(0, 1, "s")
                O(0, 2, "s")
                O(0, 3, "s")
            E(n, 0, 0, DS)
            E(n, 1, 0, DS)
            E(n, 2, 0, DS)
            if 0 < n and n + 2 < NCH:
                T(n + 2, 0, "bank2")
            keep_busy("bank1")
            E(n, 3, 0, DS)
            if 0 < n and n + 2 < NCH:
                T(n + 2, 1, "bank3")
                HC(n + 2, 0, "s")
                HC(n + 2, 1, "s")
            GR(n, "s", 0, DS)
            if n == 0:
                T(2, 0, "acc2")
                T(2, 1, "acc3")
                HC(2, 0, "s")
                HC(2, 1, "s")
            HQ(n + 1, 0, KP)
            if n == last - 1:
                S1pair(last, 0, 0, "bank0")
                S1pair(last, 2, 0, "bank1")
                S1pair(last, 0, HALF, "bank2")
                S1pair(last, 2, HALF, "bank3")
            else:
                for j in range(PACK):
                    S1full(n + 1, j)
            if n >= 1:
                GQ(n - 1, 0, DS)
            if n == last - 1:
                pass
            if 1 <= n <= CH or n == last - 1:
                for k in range(n - 1 if n <= CH else n - 2, n):
                    for r in range(PACK):
                        S2(k, r)
            PQ(n)

        PR(last, "g", 0, 448)
        for j in range(PACK):
            E(last, j, 0, HALF)
        GR(last, "s", 0, HALF)
        for j in range(PACK):
            E(last, j, HALF, DS)
        GR(last, "s", HALF, HALF + P)
        GR(last, "s", HALF + P, DS)
        PR(last, "v", 448, DM)
        GQ(last - 1, 0, DS)
        S2(last - 1, 0)
        S2(last - 1, 1)
        PQ(last)
        GQ(last, 0, HALF)
        S2(last, 0)
        S2(last, 1)
        S2(last - 1, 2)
        S2(last - 1, 3)
        GQ(last, HALF, HALF + P)
        S2(last, 2)
        GQ(last, HALF + P, DS)
        S2(last, 3)
        O(1, 0, "s")
        O(1, 1, "v")
        O(1, 2, "s")
        O(1, 3, "v")
